import numpy as np
import ml_dtypes

BF16 = ml_dtypes.bfloat16


def bf(x):
    return np.asarray(x, np.float32).astype(BF16)


def f32(x):
    return np.asarray(x, np.float32)


def f64(x):
    return np.asarray(x).astype(np.float64)


def striped(idx):
    return np.tile(idx.reshape(-1, 16).T, (8, 1))


D, S, R, N, M, H, HD = 128, 512, 8, 4096, 256, 2, 64
SCALE = 1.0 / np.sqrt(HD)


def setup_inputs():
    return {"x": bf(np.random.standard_normal((D, S))), "wq": bf(np.random.standard_normal((D, D)) / np.sqrt(D)), "wkv": bf(np.random.standard_normal((D, M)) / np.sqrt(D)), "bq": f32(0.1 * np.random.standard_normal((D, 1))), "bv": f32(0.1 * np.random.standard_normal((D, 1))), "offs": striped(np.concatenate([np.random.permutation(S) for _ in range(R)]))}


def reference(x, wq, wkv, bq, bv, offs):
    idx = offs[:16].T.reshape(-1)
    xs = f64(x)
    q = f64(wq).T @ xs + f64(bq)
    kv = f64(wkv).T @ xs[:, idx]
    kg = kv[:D].reshape(D, R, S)
    vg = kv[D:].reshape(D, R, S) + f64(bv)[:, :, None]
    sc = SCALE * (q[:, None, :] * kg).reshape(H, HD, R, S).sum(axis=1)
    e = np.exp(sc - sc.max(axis=1, keepdims=True))
    p = e / e.sum(axis=1, keepdims=True)
    p = np.repeat(p, HD, axis=0)
    return (p * vg).sum(axis=1)

@@ -1,0 +1,166 @@
+import concourse.mybir as mybir
+from concourse.masks import make_identity
+
+F32 = mybir.dt.float32
+BF16 = mybir.dt.bfloat16
+U16 = mybir.dt.uint16
+ALU = mybir.AluOpType
+ACT = mybir.ActivationFunctionType
+AX = mybir.AxisListType
+
+P = 128
+S = 512
+R = 8
+H = 2
+HD = P // H
+TB = S // P
+PIECE_COLS = S // 16
+SCALE = 0.125
+WEIGHTS = H * R
+
+FLOPS = 2 * P * (2 * P) * (R * S) + 2 * P * P * S + 4 * P * R * S
+
+BANKS = 8
+
+GPSIMD_TERMS = 4
+
+
+def bank(psum, number, shape, name):
+    return psum.tile(shape, F32, name=name, tag=f"bank{number % BANKS}")
+
+
+def tile_cantorattention_kernel(tc, x, wq, wkv, bq, bv, offs, out):
+    nc = tc.nc
+    with (
+        tc.tile_pool(name="held", bufs=1) as held,
+        tc.psum_pool(name="psum", bufs=1) as psum,
+    ):
+        wq_sb = held.tile([P, P], BF16, name="wq_sb")
+        nc.sync.dma_start(wq_sb[:], wq)
+        x_sb = held.tile([P, S], BF16, name="x_sb")
+        nc.scalar.dma_start(x_sb[:], x)
+        offsets = held.tile([P, R * PIECE_COLS], U16, name="offsets")
+        nc.sync.dma_start(offsets[:], offs)
+        wkv_sb = held.tile([P, 2 * P], BF16, name="wkv_sb")
+        nc.scalar.dma_start(wkv_sb[:], wkv)
+        bq_sb = held.tile([P, 1], F32, name="bq_sb")
+        nc.sync.dma_start(bq_sb[:], bq)
+        bv_sb = held.tile([P, 1], F32, name="bv_sb")
+        nc.scalar.dma_start(bv_sb[:], bv)
+
+        warm = held.tile([P, 1], F32, name="warm")
+        nc.vector.memset(warm[:], 0.0)
+        nc.scalar.activation(warm[:], warm[:], ACT.Exp)
+
+        head_of = held.tile([P, H], BF16, name="head_of")
+        nc.vector.memset(head_of[:], 0.0)
+        for h in range(H):
+            nc.vector.memset(head_of[h * HD : (h + 1) * HD, h : h + 1], 1.0)
+
+        identity = held.tile([P, P], BF16, name="identity")
+        make_identity(nc, identity[:])
+
+        split = held.tile([P, TB, P], BF16, name="split")
+        nc.vector.memset(split[:], 0.0)
+
+        spread = held.tile([P, R, P], BF16, name="spread")
+        nc.gpsimd.memset(spread[:], 0.0)
+        for first_row in (0, WEIGHTS):
+            nc.gpsimd.affine_select(
+                out=spread[:],
+                in_=spread[:],
+                compare_op=ALU.not_equal,
+                fill=1.0,
+                base=-first_row,
+                pattern=[[-H, R], [-1, H], [0, HD]],
+                channel_multiplier=1,
+            )
+
+        q_ps = bank(psum, R - 1, [P, S], "q_ps")
+        nc.tensor.matmul(q_ps[:], lhsT=wq_sb[:], rhs=x_sb[:], start=True, stop=True)
+        q_sb = held.tile([P, S], F32, name="q_sb")
+        nc.scalar.activation(q_sb[:], q_ps[:], ACT.Identity, bias=bq_sb[:])
+
+        qk = []
+        for r in range(R):
+            piece = offsets[:, r * PIECE_COLS : (r + 1) * PIECE_COLS]
+            k_ps = bank(psum, r, [P, S], f"k_ps{r}")
+            nc.tensor.matmul(
+                k_ps[:], lhsT=wkv_sb[:, 0:P], rhs=x_sb[:].indirect(piece), start=True, stop=True
+            )
+            qk_r = held.tile([P, S], BF16, name=f"qk{r}")
+            nc.vector.tensor_tensor(qk_r[:], k_ps[:], q_sb[:], ALU.mult)
+            qk.append(qk_r)
+
+        sc_ps = bank(psum, R - 1, [P, TB, R, H], "sc_ps")
+        for r in range(R):
+            for b in range(TB):
+                nc.tensor.matmul(
+                    sc_ps[:, b, r, :],
+                    lhsT=qk[r][:, b * P : (b + 1) * P],
+                    rhs=head_of[:],
+                    start=True,
+                    stop=True,
+                )
+
+        top = held.tile([P, TB, H], F32, name="top")
+        nc.vector.reduce_max(top[:], sc_ps[:].rearrange("t b r h -> t b h r"), axis=AX.X)
+        shifted = held.tile([P, TB, R, H], F32, name="shifted")
+        nc.vector.tensor_tensor(
+            shifted[:], sc_ps[:], top[:].unsqueeze(2).to_broadcast([P, TB, R, H]), ALU.subtract
+        )
+        e = held.tile([P, TB, R, H], F32, name="e")
+        nc.scalar.activation(e[:], shifted[:], ACT.Exp, scale=SCALE)
+        den = held.tile([P, TB, H], F32, name="den")
+        nc.vector.reduce_sum(den[:], e[:].rearrange("t b r h -> t b h r"), axis=AX.X)
+        rden = held.tile([P, TB, H], F32, name="rden")
+        nc.vector.reciprocal(rden[:], den[:])
+        rden_all_r = rden[:].unsqueeze(2).to_broadcast([P, TB, R, H])
+
+        p = held.tile([P, TB, R, H], F32, name="p")
+        nc.vector.tensor_tensor(p[:], e[:], rden_all_r, ALU.mult)
+        rounding = split[:, :, 0:WEIGHTS].rearrange("t b (r h) -> t b r h", h=H)
+        remainder = split[:, :, WEIGHTS : 2 * WEIGHTS].rearrange("t b (r h) -> t b r h", h=H)
+        nc.vector.tensor_tensor(rounding, e[:], rden_all_r, ALU.mult)
+        nc.vector.tensor_tensor(remainder, p[:], rounding, ALU.subtract)
+
+        v_sb = []
+        for r in range(R):
+            piece = offsets[:, r * PIECE_COLS : (r + 1) * PIECE_COLS]
+            v_ps = bank(psum, r, [P, S], f"v_ps{r}")
+            nc.tensor.matmul(
+                v_ps[:], lhsT=wkv_sb[:, P : 2 * P], rhs=x_sb[:].indirect(piece), start=True, stop=True
+            )
+            v_sb_r = held.tile([P, S], F32, name=f"v_sb{r}")
+            nc.scalar.activation(v_sb_r[:], v_ps[:], ACT.Identity, bias=bv_sb[:])
+            v_sb.append(v_sb_r)
+
+        turned_ps = bank(psum, 0, [P, S], "turned_ps")
+        for b in range(TB):
+            nc.tensor.matmul(
+                turned_ps[:, b * P : (b + 1) * P],
+                lhsT=split[:, b, :],
+                rhs=identity[:],
+                start=True,
+                stop=True,
+            )
+        turned = held.tile([P, S], BF16, name="turned")
+        nc.vector.tensor_copy(turned[:], turned_ps[:])
+
+        weighted = []
+        for r in range(R):
+            w_ps = bank(psum, r + 1, [P, S], f"w_ps{r}")
+            nc.tensor.matmul(w_ps[:], lhsT=spread[:, r, :], rhs=turned[:], start=True, stop=True)
+            term = held.tile([P, S], F32, name=f"term{r}")
+            nc.vector.tensor_tensor(term[:], w_ps[:], v_sb[r][:], ALU.mult)
+            weighted.append(term)
+
+        early = weighted[0]
+        for r in range(1, GPSIMD_TERMS):
+            nc.gpsimd.tensor_tensor(early[:], early[:], weighted[r][:], ALU.add)
+        late = weighted[GPSIMD_TERMS]
+        for r in range(GPSIMD_TERMS + 1, R):
+            nc.vector.tensor_tensor(late[:], late[:], weighted[r][:], ALU.add)
+        out_sb = held.tile([P, S], F32, name="out_sb")
+        nc.vector.tensor_tensor(out_sb[:], early[:], late[:], ALU.add)
+        nc.sync.dma_start(out, out_sb[:])

@@ -1,5 +1,4 @@
 import concourse.mybir as mybir
-from concourse.masks import make_identity
 
 F32 = mybir.dt.float32
 BF16 = mybir.dt.bfloat16
@@ -17,23 +16,21 @@ TB = S // P
 PIECE_COLS = S // 16
 SCALE = 0.125
 WEIGHTS = H * R
+BLOCK = 32
+QUARTERS = P // BLOCK
 
 FLOPS = 2 * P * (2 * P) * (R * S) + 2 * P * P * S + 4 * P * R * S
 
-BANKS = 8
+RING = 7
 
 GPSIMD_TERMS = 4
-
-
-def bank(psum, number, shape, name):
-    return psum.tile(shape, F32, name=name, tag=f"bank{number % BANKS}")
 
 
 def tile_cantorattention_kernel(tc, x, wq, wkv, bq, bv, offs, out):
     nc = tc.nc
     with (
         tc.tile_pool(name="held", bufs=1) as held,
-        tc.psum_pool(name="psum", bufs=1) as psum,
+        tc.psum_pool(name="psum_scores", bufs=1) as psum_scores,
     ):
         wq_sb = held.tile([P, P], BF16, name="wq_sb")
         nc.sync.dma_start(wq_sb[:], wq)
@@ -57,14 +54,8 @@ def tile_cantorattention_kernel(tc, x, wq, wkv, bq, bv, offs, out):
         for h in range(H):
             nc.vector.memset(head_of[h * HD : (h + 1) * HD, h : h + 1], 1.0)
 
-        identity = held.tile([P, P], BF16, name="identity")
-        make_identity(nc, identity[:])
-
-        split = held.tile([P, TB, P], BF16, name="split")
-        nc.vector.memset(split[:], 0.0)
-
-        spread = held.tile([P, R, P], BF16, name="spread")
-        nc.gpsimd.memset(spread[:], 0.0)
+        spread = held.tile([P, QUARTERS, R, P], BF16, name="spread")
+        nc.vector.memset(spread[:], 0.0)
         for first_row in (0, WEIGHTS):
             nc.gpsimd.affine_select(
                 out=spread[:],
@@ -72,27 +63,27 @@ def tile_cantorattention_kernel(tc, x, wq, wkv, bq, bv, offs, out):
                 compare_op=ALU.not_equal,
                 fill=1.0,
                 base=-first_row,
-                pattern=[[-H, R], [-1, H], [0, HD]],
+                pattern=[[-BLOCK, QUARTERS], [-H, R], [-1, H], [0, HD]],
                 channel_multiplier=1,
             )
 
-        q_ps = bank(psum, R - 1, [P, S], "q_ps")
-        nc.tensor.matmul(q_ps[:], lhsT=wq_sb[:], rhs=x_sb[:], start=True, stop=True)
-        q_sb = held.tile([P, S], F32, name="q_sb")
-        nc.scalar.activation(q_sb[:], q_ps[:], ACT.Identity, bias=bq_sb[:])
-
         qk = []
-        for r in range(R):
-            piece = offsets[:, r * PIECE_COLS : (r + 1) * PIECE_COLS]
-            k_ps = bank(psum, r, [P, S], f"k_ps{r}")
-            nc.tensor.matmul(
-                k_ps[:], lhsT=wkv_sb[:, 0:P], rhs=x_sb[:].indirect(piece), start=True, stop=True
-            )
-            qk_r = held.tile([P, S], BF16, name=f"qk{r}")
-            nc.vector.tensor_tensor(qk_r[:], k_ps[:], q_sb[:], ALU.mult)
-            qk.append(qk_r)
+        with tc.psum_pool(name="psum_keys", bufs=RING) as psum_keys:
+            q_ps = psum_keys.tile([P, S], F32, name="q_ps", tag="keys")
+            nc.tensor.matmul(q_ps[:], lhsT=wq_sb[:], rhs=x_sb[:], start=True, stop=True)
+            q_sb = held.tile([P, S], F32, name="q_sb")
+            nc.scalar.activation(q_sb[:], q_ps[:], ACT.Identity, bias=bq_sb[:])
+            for r in range(R):
+                piece = offsets[:, r * PIECE_COLS : (r + 1) * PIECE_COLS]
+                k_ps = psum_keys.tile([P, S], F32, name="k_ps", tag="keys")
+                nc.tensor.matmul(
+                    k_ps[:], lhsT=wkv_sb[:, 0:P], rhs=x_sb[:].indirect(piece), start=True, stop=True
+                )
+                qk_r = held.tile([P, S], BF16, name=f"qk{r}")
+                nc.vector.tensor_tensor(qk_r[:], k_ps[:], q_sb[:], ALU.mult)
+                qk.append(qk_r)
 
-        sc_ps = bank(psum, R - 1, [P, TB, R, H], "sc_ps")
+        sc_ps = psum_scores.tile([P, TB, R, H], F32, name="sc_ps")
         for r in range(R):
             for b in range(TB):
                 nc.tensor.matmul(
@@ -119,41 +110,46 @@ def tile_cantorattention_kernel(tc, x, wq, wkv, bq, bv, offs, out):
 
         p = held.tile([P, TB, R, H], F32, name="p")
         nc.vector.tensor_tensor(p[:], e[:], rden_all_r, ALU.mult)
-        rounding = split[:, :, 0:WEIGHTS].rearrange("t b (r h) -> t b r h", h=H)
-        remainder = split[:, :, WEIGHTS : 2 * WEIGHTS].rearrange("t b (r h) -> t b r h", h=H)
+        split = held.tile([P, TB * BLOCK], BF16, name="split", align_bytes=64)
+        parts = split[:].rearrange("t (b k) -> t b k", b=TB)
+        rounding = parts[:, :, 0:WEIGHTS].rearrange("t b (r h) -> t b r h", h=H)
+        remainder = parts[:, :, WEIGHTS : 2 * WEIGHTS].rearrange("t b (r h) -> t b r h", h=H)
         nc.vector.tensor_tensor(rounding, e[:], rden_all_r, ALU.mult)
         nc.vector.tensor_tensor(remainder, p[:], rounding, ALU.subtract)
 
-        v_sb = []
-        for r in range(R):
-            piece = offsets[:, r * PIECE_COLS : (r + 1) * PIECE_COLS]
-            v_ps = bank(psum, r, [P, S], f"v_ps{r}")
-            nc.tensor.matmul(
-                v_ps[:], lhsT=wkv_sb[:, P : 2 * P], rhs=x_sb[:].indirect(piece), start=True, stop=True
-            )
-            v_sb_r = held.tile([P, S], F32, name=f"v_sb{r}")
-            nc.scalar.activation(v_sb_r[:], v_ps[:], ACT.Identity, bias=bv_sb[:])
-            v_sb.append(v_sb_r)
+        turned = held.tile([P, TB * BLOCK], BF16, name="turned", align_bytes=64)
+        nc.vector.transpose(turned[:], split[:])
 
-        turned_ps = bank(psum, 0, [P, S], "turned_ps")
-        for b in range(TB):
-            nc.tensor.matmul(
-                turned_ps[:, b * P : (b + 1) * P],
-                lhsT=split[:, b, :],
-                rhs=identity[:],
-                start=True,
-                stop=True,
-            )
-        turned = held.tile([P, S], BF16, name="turned")
-        nc.vector.tensor_copy(turned[:], turned_ps[:])
+        with tc.psum_pool(name="psum_values", bufs=RING) as psum_values:
+            v_sb = []
+            for r in range(R):
+                piece = offsets[:, r * PIECE_COLS : (r + 1) * PIECE_COLS]
+                v_ps = psum_values.tile([P, S], F32, name="v_ps", tag="values")
+                nc.tensor.matmul(
+                    v_ps[:],
+                    lhsT=wkv_sb[:, P : 2 * P],
+                    rhs=x_sb[:].indirect(piece),
+                    start=True,
+                    stop=True,
+                )
+                v_sb_r = held.tile([P, S], F32, name=f"v_sb{r}")
+                nc.scalar.activation(v_sb_r[:], v_ps[:], ACT.Identity, bias=bv_sb[:])
+                v_sb.append(v_sb_r)
 
-        weighted = []
-        for r in range(R):
-            w_ps = bank(psum, r + 1, [P, S], f"w_ps{r}")
-            nc.tensor.matmul(w_ps[:], lhsT=spread[:, r, :], rhs=turned[:], start=True, stop=True)
-            term = held.tile([P, S], F32, name=f"term{r}")
-            nc.vector.tensor_tensor(term[:], w_ps[:], v_sb[r][:], ALU.mult)
-            weighted.append(term)
+            weighted = []
+            for r in range(R):
+                w_ps = psum_values.tile([P, S], F32, name="w_ps", tag="values")
+                for g in range(QUARTERS):
+                    nc.tensor.matmul(
+                        w_ps[:].rearrange("c (b g j) -> c b g j", b=TB, g=QUARTERS)[:, :, g, :],
+                        lhsT=spread[:, g, r, :],
+                        rhs=turned[:].rearrange("k (b j) -> k b j", b=TB),
+                        start=True,
+                        stop=True,
+                    )
+                term = held.tile([P, S], F32, name=f"term{r}")
+                nc.vector.tensor_tensor(term[:], w_ps[:], v_sb[r][:], ALU.mult)
+                weighted.append(term)
 
         early = weighted[0]
         for r in range(1, GPSIMD_TERMS):

@@ -23,6 +23,8 @@ FLOPS = 2 * P * (2 * P) * (R * S) + 2 * P * P * S + 4 * P * R * S
 
 RING = 7
 
+VIA_GPSIMD = 3
+
 GPSIMD_TERMS = 4
 
 
@@ -54,18 +56,26 @@ def tile_cantorattention_kernel(tc, x, wq, wkv, bq, bv, offs, out):
         for h in range(H):
             nc.vector.memset(head_of[h * HD : (h + 1) * HD, h : h + 1], 1.0)
 
-        spread = held.tile([P, QUARTERS, R, P], BF16, name="spread")
-        nc.vector.memset(spread[:], 0.0)
+        pick = held.tile([P, QUARTERS, WEIGHTS], BF16, name="pick")
+        nc.gpsimd.memset(pick[:], 0.0)
         for first_row in (0, WEIGHTS):
             nc.gpsimd.affine_select(
-                out=spread[:],
-                in_=spread[:],
+                out=pick[:],
+                in_=pick[:],
                 compare_op=ALU.not_equal,
                 fill=1.0,
                 base=-first_row,
-                pattern=[[-BLOCK, QUARTERS], [-H, R], [-1, H], [0, HD]],
+                pattern=[[-BLOCK, QUARTERS], [-1, WEIGHTS]],
                 channel_multiplier=1,
             )
+        spread = held.tile([P, QUARTERS, R, P], BF16, name="spread")
+        nc.gpsimd.tensor_copy(
+            spread[:].rearrange("k g r (h c) -> k (g r h) c", h=H),
+            pick[:]
+            .rearrange("k g w -> k (g w)")
+            .unsqueeze(2)
+            .to_broadcast([P, QUARTERS * WEIGHTS, HD]),
+        )
 
         qk = []
         with tc.psum_pool(name="psum_keys", bufs=RING) as psum_keys:
@@ -79,8 +89,14 @@ def tile_cantorattention_kernel(tc, x, wq, wkv, bq, bv, offs, out):
                 nc.tensor.matmul(
                     k_ps[:], lhsT=wkv_sb[:, 0:P], rhs=x_sb[:].indirect(piece), start=True, stop=True
                 )
-                qk_r = held.tile([P, S], BF16, name=f"qk{r}")
-                nc.vector.tensor_tensor(qk_r[:], k_ps[:], q_sb[:], ALU.mult)
+                slot = "k_sb" if r == R - 1 else f"qk{r}"
+                qk_r = held.tile([P, S], BF16, name=f"qk{r}", tag=slot)
+                if r == VIA_GPSIMD:
+                    k_sb = held.tile([P, S], F32, name="k_sb")
+                    nc.scalar.copy(k_sb[:], k_ps[:])
+                    nc.gpsimd.tensor_tensor(qk_r[:], k_sb[:], q_sb[:], ALU.mult)
+                else:
+                    nc.vector.tensor_tensor(qk_r[:], k_ps[:], q_sb[:], ALU.mult)
                 qk.append(qk_r)
 
         sc_ps = psum_scores.tile([P, TB, R, H], F32, name="sc_ps")

@@ -1,4 +1,5 @@
 import concourse.mybir as mybir
+from concourse.masks import make_identity
 
 F32 = mybir.dt.float32
 BF16 = mybir.dt.bfloat16
@@ -25,7 +26,8 @@ RING = 7
 
 VIA_GPSIMD = 3
 
-GPSIMD_TERMS = 4
+GPSIMD_TERMS = 3
+TENSOR_TERMS = 3
 
 
 def tile_cantorattention_kernel(tc, x, wq, wkv, bq, bv, offs, out):
@@ -76,6 +78,9 @@ def tile_cantorattention_kernel(tc, x, wq, wkv, bq, bv, offs, out):
             .unsqueeze(2)
             .to_broadcast([P, QUARTERS * WEIGHTS, HD]),
         )
+
+        identity = held.tile([P, P], F32, name="identity")
+        make_identity(nc, identity[:])
 
         qk = []
         with tc.psum_pool(name="psum_keys", bufs=RING) as psum_keys:
@@ -167,12 +172,23 @@ def tile_cantorattention_kernel(tc, x, wq, wkv, bq, bv, offs, out):
                 nc.vector.tensor_tensor(term[:], w_ps[:], v_sb[r][:], ALU.mult)
                 weighted.append(term)
 
-        early = weighted[0]
-        for r in range(1, GPSIMD_TERMS):
-            nc.gpsimd.tensor_tensor(early[:], early[:], weighted[r][:], ALU.add)
-        late = weighted[GPSIMD_TERMS]
-        for r in range(GPSIMD_TERMS + 1, R):
-            nc.vector.tensor_tensor(late[:], late[:], weighted[r][:], ALU.add)
-        out_sb = held.tile([P, S], F32, name="out_sb")
-        nc.vector.tensor_tensor(out_sb[:], early[:], late[:], ALU.add)
+            early = weighted[0]
+            for r in range(1, GPSIMD_TERMS):
+                nc.gpsimd.tensor_tensor(early[:], early[:], weighted[r][:], ALU.add)
+            middle_ps = psum_values.tile([P, S], F32, name="middle_ps", tag="values")
+            first, last = GPSIMD_TERMS, GPSIMD_TERMS + TENSOR_TERMS - 1
+            for r in range(first, last + 1):
+                nc.tensor.matmul(
+                    middle_ps[:],
+                    lhsT=identity[:],
+                    rhs=weighted[r][:],
+                    start=(r == first),
+                    stop=(r == last),
+                )
+            late = weighted[last + 1]
+            for r in range(last + 2, R):
+                nc.vector.tensor_tensor(late[:], late[:], weighted[r][:], ALU.add)
+            nc.vector.tensor_tensor(late[:], late[:], early[:], ALU.add)
+            out_sb = held.tile([P, S], F32, name="out_sb")
+            nc.vector.tensor_tensor(out_sb[:], middle_ps[:], late[:], ALU.add)
         nc.sync.dma_start(out, out_sb[:])

@@ -26,6 +26,8 @@ RING = 7
 
 VIA_GPSIMD = 3
 
+VALUES_IN_KEYS_RUN = 1
+
 GPSIMD_TERMS = 3
 TENSOR_TERMS = 3
 
@@ -104,6 +106,21 @@ def tile_cantorattention_kernel(tc, x, wq, wkv, bq, bv, offs, out):
                     nc.vector.tensor_tensor(qk_r[:], k_ps[:], q_sb[:], ALU.mult)
                 qk.append(qk_r)
 
+            v_sb = []
+            for r in range(VALUES_IN_KEYS_RUN):
+                piece = offsets[:, r * PIECE_COLS : (r + 1) * PIECE_COLS]
+                v_ps = psum_keys.tile([P, S], F32, name="v_ps", tag="keys")
+                nc.tensor.matmul(
+                    v_ps[:],
+                    lhsT=wkv_sb[:, P : 2 * P],
+                    rhs=x_sb[:].indirect(piece),
+                    start=True,
+                    stop=True,
+                )
+                v_sb_r = held.tile([P, S], F32, name=f"v_sb{r}")
+                nc.scalar.activation(v_sb_r[:], v_ps[:], ACT.Identity, bias=bv_sb[:])
+                v_sb.append(v_sb_r)
+
         sc_ps = psum_scores.tile([P, TB, R, H], F32, name="sc_ps")
         for r in range(R):
             for b in range(TB):
@@ -142,8 +159,7 @@ def tile_cantorattention_kernel(tc, x, wq, wkv, bq, bv, offs, out):
         nc.vector.transpose(turned[:], split[:])
 
         with tc.psum_pool(name="psum_values", bufs=RING) as psum_values:
-            v_sb = []
-            for r in range(R):
+            for r in range(VALUES_IN_KEYS_RUN, R):
                 piece = offsets[:, r * PIECE_COLS : (r + 1) * PIECE_COLS]
                 v_ps = psum_values.tile([P, S], F32, name="v_ps", tag="values")
                 nc.tensor.matmul(

@@ -206,5 +206,10 @@ def tile_cantorattention_kernel(tc, x, wq, wkv, bq, bv, offs, out):
                 nc.vector.tensor_tensor(late[:], late[:], weighted[r][:], ALU.add)
             nc.vector.tensor_tensor(late[:], late[:], early[:], ALU.add)
             out_sb = held.tile([P, S], F32, name="out_sb")
-            nc.vector.tensor_tensor(out_sb[:], middle_ps[:], late[:], ALU.add)
-        nc.sync.dma_start(out, out_sb[:])
+            half = S // 2
+            for first_token, queue in ((0, nc.sync), (half, nc.scalar)):
+                tokens = slice(first_token, first_token + half)
+                nc.vector.tensor_tensor(
+                    out_sb[:, tokens], middle_ps[:, tokens], late[:, tokens], ALU.add
+                )
+                queue.dma_start(out[:, tokens], out_sb[:, tokens])

@@ -159,7 +159,7 @@ def tile_cantorattention_kernel(tc, x, wq, wkv, bq, bv, offs, out):
         nc.vector.transpose(turned[:], split[:])
 
         with tc.psum_pool(name="psum_values", bufs=RING) as psum_values:
-            for r in range(VALUES_IN_KEYS_RUN, R):
+            def gather_values(r):
                 piece = offsets[:, r * PIECE_COLS : (r + 1) * PIECE_COLS]
                 v_ps = psum_values.tile([P, S], F32, name="v_ps", tag="values")
                 nc.tensor.matmul(
@@ -173,8 +173,13 @@ def tile_cantorattention_kernel(tc, x, wq, wkv, bq, bv, offs, out):
                 nc.scalar.activation(v_sb_r[:], v_ps[:], ACT.Identity, bias=bv_sb[:])
                 v_sb.append(v_sb_r)
 
+            for r in range(VALUES_IN_KEYS_RUN, R - 1):
+                gather_values(r)
+
             weighted = []
             for r in range(R):
+                if r == R - 2:
+                    gather_values(R - 1)
                 w_ps = psum_values.tile([P, S], F32, name="w_ps", tag="values")
                 for g in range(QUARTERS):
                     nc.tensor.matmul(

@@ -16,20 +16,17 @@ HD = P // H
 TB = S // P
 PIECE_COLS = S // 16
 SCALE = 0.125
-WEIGHTS = H * R
-BLOCK = 32
-QUARTERS = P // BLOCK
 
 FLOPS = 2 * P * (2 * P) * (R * S) + 2 * P * P * S + 4 * P * R * S
 
-RING = 7
+KEY_BANKS = 7
+VALUE_BANKS = 3
+TURNED_BANKS = 2
+SUM_BANKS = 2
 
 VIA_GPSIMD = 3
 
 VALUES_IN_KEYS_RUN = 1
-
-GPSIMD_TERMS = 3
-TENSOR_TERMS = 3
 
 
 def tile_cantorattention_kernel(tc, x, wq, wkv, bq, bv, offs, out):
@@ -60,32 +57,12 @@ def tile_cantorattention_kernel(tc, x, wq, wkv, bq, bv, offs, out):
         for h in range(H):
             nc.vector.memset(head_of[h * HD : (h + 1) * HD, h : h + 1], 1.0)
 
-        pick = held.tile([P, QUARTERS, WEIGHTS], BF16, name="pick")
-        nc.gpsimd.memset(pick[:], 0.0)
-        for first_row in (0, WEIGHTS):
-            nc.gpsimd.affine_select(
-                out=pick[:],
-                in_=pick[:],
-                compare_op=ALU.not_equal,
-                fill=1.0,
-                base=-first_row,
-                pattern=[[-BLOCK, QUARTERS], [-1, WEIGHTS]],
-                channel_multiplier=1,
-            )
-        spread = held.tile([P, QUARTERS, R, P], BF16, name="spread")
-        nc.gpsimd.tensor_copy(
-            spread[:].rearrange("k g r (h c) -> k (g r h) c", h=H),
-            pick[:]
-            .rearrange("k g w -> k (g w)")
-            .unsqueeze(2)
-            .to_broadcast([P, QUARTERS * WEIGHTS, HD]),
-        )
-
         identity = held.tile([P, P], F32, name="identity")
         make_identity(nc, identity[:])
 
         qk = []
-        with tc.psum_pool(name="psum_keys", bufs=RING) as psum_keys:
+        v_sb = []
+        with tc.psum_pool(name="psum_keys", bufs=KEY_BANKS) as psum_keys:
             q_ps = psum_keys.tile([P, S], F32, name="q_ps", tag="keys")
             nc.tensor.matmul(q_ps[:], lhsT=wq_sb[:], rhs=x_sb[:], start=True, stop=True)
             q_sb = held.tile([P, S], F32, name="q_sb")
@@ -106,19 +83,14 @@ def tile_cantorattention_kernel(tc, x, wq, wkv, bq, bv, offs, out):
                     nc.vector.tensor_tensor(qk_r[:], k_ps[:], q_sb[:], ALU.mult)
                 qk.append(qk_r)
 
-            v_sb = []
             for r in range(VALUES_IN_KEYS_RUN):
                 piece = offsets[:, r * PIECE_COLS : (r + 1) * PIECE_COLS]
                 v_ps = psum_keys.tile([P, S], F32, name="v_ps", tag="keys")
                 nc.tensor.matmul(
-                    v_ps[:],
-                    lhsT=wkv_sb[:, P : 2 * P],
-                    rhs=x_sb[:].indirect(piece),
-                    start=True,
-                    stop=True,
+                    v_ps[:], lhsT=wkv_sb[:, P : 2 * P], rhs=x_sb[:].indirect(piece), start=True, stop=True
                 )
                 v_sb_r = held.tile([P, S], F32, name=f"v_sb{r}")
-                nc.scalar.activation(v_sb_r[:], v_ps[:], ACT.Identity, bias=bv_sb[:])
+                nc.scalar.copy(v_sb_r[:], v_ps[:])
                 v_sb.append(v_sb_r)
 
         sc_ps = psum_scores.tile([P, TB, R, H], F32, name="sc_ps")
@@ -134,7 +106,7 @@ def tile_cantorattention_kernel(tc, x, wq, wkv, bq, bv, offs, out):
 
         top = held.tile([P, TB, H], F32, name="top")
         nc.vector.reduce_max(top[:], sc_ps[:].rearrange("t b r h -> t b h r"), axis=AX.X)
-        shifted = held.tile([P, TB, R, H], F32, name="shifted")
+        shifted = held.tile([P, TB, R, H], F32, name="shifted", tag=f"v_sb{VALUES_IN_KEYS_RUN}")
         nc.vector.tensor_tensor(
             shifted[:], sc_ps[:], top[:].unsqueeze(2).to_broadcast([P, TB, R, H]), ALU.subtract
         )
@@ -144,77 +116,57 @@ def tile_cantorattention_kernel(tc, x, wq, wkv, bq, bv, offs, out):
         nc.vector.reduce_sum(den[:], e[:].rearrange("t b r h -> t b h r"), axis=AX.X)
         rden = held.tile([P, TB, H], F32, name="rden")
         nc.vector.reciprocal(rden[:], den[:])
-        rden_all_r = rden[:].unsqueeze(2).to_broadcast([P, TB, R, H])
 
-        p = held.tile([P, TB, R, H], F32, name="p")
-        nc.vector.tensor_tensor(p[:], e[:], rden_all_r, ALU.mult)
-        split = held.tile([P, TB * BLOCK], BF16, name="split", align_bytes=64)
-        parts = split[:].rearrange("t (b k) -> t b k", b=TB)
-        rounding = parts[:, :, 0:WEIGHTS].rearrange("t b (r h) -> t b r h", h=H)
-        remainder = parts[:, :, WEIGHTS : 2 * WEIGHTS].rearrange("t b (r h) -> t b r h", h=H)
-        nc.vector.tensor_tensor(rounding, e[:], rden_all_r, ALU.mult)
-        nc.vector.tensor_tensor(remainder, p[:], rounding, ALU.subtract)
-
-        turned = held.tile([P, TB * BLOCK], BF16, name="turned", align_bytes=64)
-        nc.vector.transpose(turned[:], split[:])
-
-        with tc.psum_pool(name="psum_values", bufs=RING) as psum_values:
-            def gather_values(r):
-                piece = offsets[:, r * PIECE_COLS : (r + 1) * PIECE_COLS]
-                v_ps = psum_values.tile([P, S], F32, name="v_ps", tag="values")
-                nc.tensor.matmul(
-                    v_ps[:],
-                    lhsT=wkv_sb[:, P : 2 * P],
-                    rhs=x_sb[:].indirect(piece),
-                    start=True,
-                    stop=True,
-                )
-                v_sb_r = held.tile([P, S], F32, name=f"v_sb{r}")
-                nc.scalar.activation(v_sb_r[:], v_ps[:], ACT.Identity, bias=bv_sb[:])
-                v_sb.append(v_sb_r)
-
-            for r in range(VALUES_IN_KEYS_RUN, R - 1):
-                gather_values(r)
-
-            weighted = []
+        with (
+            tc.psum_pool(name="psum_values", bufs=VALUE_BANKS) as psum_values,
+            tc.psum_pool(name="psum_turned", bufs=TURNED_BANKS) as psum_turned,
+            tc.psum_pool(name="psum_sums", bufs=SUM_BANKS) as psum_sums,
+        ):
+            sums = [held.tile([P, P], F32, name=f"sums{b}") for b in range(TB)]
             for r in range(R):
-                if r == R - 2:
-                    gather_values(R - 1)
-                w_ps = psum_values.tile([P, S], F32, name="w_ps", tag="values")
-                for g in range(QUARTERS):
+                if r >= VALUES_IN_KEYS_RUN:
+                    piece = offsets[:, r * PIECE_COLS : (r + 1) * PIECE_COLS]
+                    v_ps = psum_values.tile([P, S], F32, name="v_ps")
                     nc.tensor.matmul(
-                        w_ps[:].rearrange("c (b g j) -> c b g j", b=TB, g=QUARTERS)[:, :, g, :],
-                        lhsT=spread[:, g, r, :],
-                        rhs=turned[:].rearrange("k (b j) -> k b j", b=TB),
+                        v_ps[:],
+                        lhsT=wkv_sb[:, P : 2 * P],
+                        rhs=x_sb[:].indirect(piece),
                         start=True,
                         stop=True,
                     )
-                term = held.tile([P, S], F32, name=f"term{r}")
-                nc.vector.tensor_tensor(term[:], w_ps[:], v_sb[r][:], ALU.mult)
-                weighted.append(term)
+                    v_sb_r = held.tile([P, S], F32, name=f"v_sb{r}")
+                    nc.scalar.copy(v_sb_r[:], v_ps[:])
+                    v_sb.append(v_sb_r)
+                turned = psum_turned.tile([P, TB, P], F32, name="turned")
+                for b in range(TB):
+                    nc.tensor.transpose(turned[:, b, :], v_sb[r][:, b * P : (b + 1) * P], identity[:])
+                for b in range(TB):
+                    for h in range(H):
+                        channels = slice(h * HD, (h + 1) * HD)
+                        weight = e[:, b, r, h : h + 1]
+                        if r == 0:
+                            nc.vector.tensor_scalar(
+                                sums[b][:, channels], turned[:, b, channels], weight, None, ALU.mult
+                            )
+                        else:
+                            nc.vector.scalar_tensor_tensor(
+                                sums[b][:, channels],
+                                turned[:, b, channels],
+                                weight,
+                                sums[b][:, channels],
+                                ALU.mult,
+                                ALU.add,
+                            )
 
-            early = weighted[0]
-            for r in range(1, GPSIMD_TERMS):
-                nc.gpsimd.tensor_tensor(early[:], early[:], weighted[r][:], ALU.add)
-            middle_ps = psum_values.tile([P, S], F32, name="middle_ps", tag="values")
-            first, last = GPSIMD_TERMS, GPSIMD_TERMS + TENSOR_TERMS - 1
-            for r in range(first, last + 1):
-                nc.tensor.matmul(
-                    middle_ps[:],
-                    lhsT=identity[:],
-                    rhs=weighted[r][:],
-                    start=(r == first),
-                    stop=(r == last),
-                )
-            late = weighted[last + 1]
-            for r in range(last + 2, R):
-                nc.vector.tensor_tensor(late[:], late[:], weighted[r][:], ALU.add)
-            nc.vector.tensor_tensor(late[:], late[:], early[:], ALU.add)
-            out_sb = held.tile([P, S], F32, name="out_sb")
-            half = S // 2
-            for first_token, queue in ((0, nc.sync), (half, nc.scalar)):
-                tokens = slice(first_token, first_token + half)
-                nc.vector.tensor_tensor(
-                    out_sb[:, tokens], middle_ps[:, tokens], late[:, tokens], ALU.add
-                )
-                queue.dma_start(out[:, tokens], out_sb[:, tokens])
+            for b in range(TB):
+                divided = held.tile([P, P], F32, name=f"divided{b}")
+                for h in range(H):
+                    channels = slice(h * HD, (h + 1) * HD)
+                    nc.scalar.activation(
+                        divided[:, channels], sums[b][:, channels], ACT.Copy, scale=rden[:, b, h : h + 1]
+                    )
+                sums_ps = psum_sums.tile([P, P], F32, name="sums_ps")
+                nc.tensor.transpose(sums_ps[:], divided[:], identity[:])
+                out_sb = held.tile([P, P], F32, name=f"out_sb{b}")
+                nc.scalar.activation(out_sb[:], sums_ps[:], ACT.Identity, bias=bv_sb[:])
+                nc.sync.dma_start(out[:, b * P : (b + 1) * P], out_sb[:])

@@ -21,12 +21,11 @@ FLOPS = 2 * P * (2 * P) * (R * S) + 2 * P * P * S + 4 * P * R * S
 
 KEY_BANKS = 7
 VALUE_BANKS = 3
-TURNED_BANKS = 2
-SUM_BANKS = 2
+TURNED_BANKS = 4
+
+AHEAD = 2
 
 VIA_GPSIMD = 3
-
-VALUES_IN_KEYS_RUN = 1
 
 
 def tile_cantorattention_kernel(tc, x, wq, wkv, bq, bv, offs, out):
@@ -60,8 +59,14 @@ def tile_cantorattention_kernel(tc, x, wq, wkv, bq, bv, offs, out):
         identity = held.tile([P, P], F32, name="identity")
         make_identity(nc, identity[:])
 
+        def gather_values(r, v_ps, v_sb):
+            piece = offsets[:, r * PIECE_COLS : (r + 1) * PIECE_COLS]
+            nc.tensor.matmul(
+                v_ps[:], lhsT=wkv_sb[:, P : 2 * P], rhs=x_sb[:].indirect(piece), start=True, stop=True
+            )
+            nc.scalar.copy(v_sb, v_ps[:])
+
         qk = []
-        v_sb = []
         with tc.psum_pool(name="psum_keys", bufs=KEY_BANKS) as psum_keys:
             q_ps = psum_keys.tile([P, S], F32, name="q_ps", tag="keys")
             nc.tensor.matmul(q_ps[:], lhsT=wq_sb[:], rhs=x_sb[:], start=True, stop=True)
@@ -83,15 +88,9 @@ def tile_cantorattention_kernel(tc, x, wq, wkv, bq, bv, offs, out):
                     nc.vector.tensor_tensor(qk_r[:], k_ps[:], q_sb[:], ALU.mult)
                 qk.append(qk_r)
 
-            for r in range(VALUES_IN_KEYS_RUN):
-                piece = offsets[:, r * PIECE_COLS : (r + 1) * PIECE_COLS]
-                v_ps = psum_keys.tile([P, S], F32, name="v_ps", tag="keys")
-                nc.tensor.matmul(
-                    v_ps[:], lhsT=wkv_sb[:, P : 2 * P], rhs=x_sb[:].indirect(piece), start=True, stop=True
-                )
-                v_sb_r = held.tile([P, S], F32, name=f"v_sb{r}")
-                nc.scalar.copy(v_sb_r[:], v_ps[:])
-                v_sb.append(v_sb_r)
+            first_v_ps = psum_keys.tile([P, S], F32, name="first_v_ps", tag="keys")
+            first_values = held.tile([P, S], F32, name="first_values")
+            gather_values(0, first_v_ps, first_values[:])
 
         sc_ps = psum_scores.tile([P, TB, R, H], F32, name="sc_ps")
         for r in range(R):
@@ -106,7 +105,7 @@ def tile_cantorattention_kernel(tc, x, wq, wkv, bq, bv, offs, out):
 
         top = held.tile([P, TB, H], F32, name="top")
         nc.vector.reduce_max(top[:], sc_ps[:].rearrange("t b r h -> t b h r"), axis=AX.X)
-        shifted = held.tile([P, TB, R, H], F32, name="shifted", tag=f"v_sb{VALUES_IN_KEYS_RUN}")
+        shifted = held.tile([P, TB, R, H], F32, name="shifted", tag="shifted_then_values")
         nc.vector.tensor_tensor(
             shifted[:], sc_ps[:], top[:].unsqueeze(2).to_broadcast([P, TB, R, H]), ALU.subtract
         )
@@ -116,34 +115,34 @@ def tile_cantorattention_kernel(tc, x, wq, wkv, bq, bv, offs, out):
         nc.vector.reduce_sum(den[:], e[:].rearrange("t b r h -> t b h r"), axis=AX.X)
         rden = held.tile([P, TB, H], F32, name="rden")
         nc.vector.reciprocal(rden[:], den[:])
+        p = held.tile([P, TB, R, H], F32, name="p")
+        nc.vector.tensor_tensor(
+            p[:], e[:], rden[:].unsqueeze(2).to_broadcast([P, TB, R, H]), ALU.mult
+        )
 
         with (
             tc.psum_pool(name="psum_values", bufs=VALUE_BANKS) as psum_values,
             tc.psum_pool(name="psum_turned", bufs=TURNED_BANKS) as psum_turned,
-            tc.psum_pool(name="psum_sums", bufs=SUM_BANKS) as psum_sums,
         ):
+            later_values = held.tile(
+                [P, R - 1, S], F32, name="later_values", tag="shifted_then_values"
+            )
+            values = [first_values[:]] + [later_values[:, r - 1, :] for r in range(1, R)]
             sums = [held.tile([P, P], F32, name=f"sums{b}") for b in range(TB)]
-            for r in range(R):
-                if r >= VALUES_IN_KEYS_RUN:
-                    piece = offsets[:, r * PIECE_COLS : (r + 1) * PIECE_COLS]
+            for step in range(1, R + AHEAD):
+                if step < R:
                     v_ps = psum_values.tile([P, S], F32, name="v_ps")
-                    nc.tensor.matmul(
-                        v_ps[:],
-                        lhsT=wkv_sb[:, P : 2 * P],
-                        rhs=x_sb[:].indirect(piece),
-                        start=True,
-                        stop=True,
-                    )
-                    v_sb_r = held.tile([P, S], F32, name=f"v_sb{r}")
-                    nc.scalar.copy(v_sb_r[:], v_ps[:])
-                    v_sb.append(v_sb_r)
-                turned = psum_turned.tile([P, TB, P], F32, name="turned")
+                    gather_values(step, v_ps, values[step])
+                r = step - AHEAD
+                if r < 0:
+                    continue
+                turned = psum_turned.tile([P, TB, P], F32, name="turned", tag="turned")
                 for b in range(TB):
-                    nc.tensor.transpose(turned[:, b, :], v_sb[r][:, b * P : (b + 1) * P], identity[:])
+                    nc.tensor.transpose(turned[:, b, :], values[r][:, b * P : (b + 1) * P], identity[:])
                 for b in range(TB):
                     for h in range(H):
                         channels = slice(h * HD, (h + 1) * HD)
-                        weight = e[:, b, r, h : h + 1]
+                        weight = p[:, b, r, h : h + 1]
                         if r == 0:
                             nc.vector.tensor_scalar(
                                 sums[b][:, channels], turned[:, b, channels], weight, None, ALU.mult
@@ -159,14 +158,11 @@ def tile_cantorattention_kernel(tc, x, wq, wkv, bq, bv, offs, out):
                             )
 
             for b in range(TB):
-                divided = held.tile([P, P], F32, name=f"divided{b}")
-                for h in range(H):
-                    channels = slice(h * HD, (h + 1) * HD)
-                    nc.scalar.activation(
-                        divided[:, channels], sums[b][:, channels], ACT.Copy, scale=rden[:, b, h : h + 1]
-                    )
-                sums_ps = psum_sums.tile([P, P], F32, name="sums_ps")
-                nc.tensor.transpose(sums_ps[:], divided[:], identity[:])
+                sums_ps = psum_turned.tile([P, P], F32, name="sums_ps", tag="turned")
+                nc.tensor.transpose(sums_ps[:], sums[b][:], identity[:])
                 out_sb = held.tile([P, P], F32, name=f"out_sb{b}")
-                nc.scalar.activation(out_sb[:], sums_ps[:], ACT.Identity, bias=bv_sb[:])
+                if b % 2 == 0:
+                    nc.scalar.activation(out_sb[:], sums_ps[:], ACT.Identity, bias=bv_sb[:])
+                else:
+                    nc.vector.tensor_scalar(out_sb[:], sums_ps[:], bv_sb[:], None, ALU.add)
                 nc.sync.dma_start(out[:, b * P : (b + 1) * P], out_sb[:])

@@ -23,6 +23,7 @@ KEY_BANKS = 7
 VALUE_BANKS = 3
 TURNED_BANKS = 4
 
+TURNED_TOGETHER = 2
 AHEAD = 2
 
 VIA_GPSIMD = 3
@@ -129,33 +130,38 @@ def tile_cantorattention_kernel(tc, x, wq, wkv, bq, bv, offs, out):
             )
             values = [first_values[:]] + [later_values[:, r - 1, :] for r in range(1, R)]
             sums = [held.tile([P, P], F32, name=f"sums{b}") for b in range(TB)]
-            for step in range(1, R + AHEAD):
-                if step < R:
+            gathered = 1
+            for first in range(0, R, TURNED_TOGETHER):
+                pieces = range(first, first + TURNED_TOGETHER)
+                for r in range(gathered, min(first + TURNED_TOGETHER + AHEAD, R)):
                     v_ps = psum_values.tile([P, S], F32, name="v_ps")
-                    gather_values(step, v_ps, values[step])
-                r = step - AHEAD
-                if r < 0:
-                    continue
-                turned = psum_turned.tile([P, TB, P], F32, name="turned", tag="turned")
-                for b in range(TB):
-                    nc.tensor.transpose(turned[:, b, :], values[r][:, b * P : (b + 1) * P], identity[:])
-                for b in range(TB):
-                    for h in range(H):
-                        channels = slice(h * HD, (h + 1) * HD)
-                        weight = p[:, b, r, h : h + 1]
-                        if r == 0:
-                            nc.vector.tensor_scalar(
-                                sums[b][:, channels], turned[:, b, channels], weight, None, ALU.mult
-                            )
-                        else:
-                            nc.vector.scalar_tensor_tensor(
-                                sums[b][:, channels],
-                                turned[:, b, channels],
-                                weight,
-                                sums[b][:, channels],
-                                ALU.mult,
-                                ALU.add,
-                            )
+                    gather_values(r, v_ps, values[r])
+                    gathered = r + 1
+                turned = {}
+                for r in pieces:
+                    turned[r] = psum_turned.tile([P, TB, P], F32, name="turned", tag="turned")
+                    for b in range(TB):
+                        nc.tensor.transpose(
+                            turned[r][:, b, :], values[r][:, b * P : (b + 1) * P], identity[:]
+                        )
+                for r in pieces:
+                    for b in range(TB):
+                        for h in range(H):
+                            channels = slice(h * HD, (h + 1) * HD)
+                            weight = p[:, b, r, h : h + 1]
+                            if r == 0:
+                                nc.vector.tensor_scalar(
+                                    sums[b][:, channels], turned[r][:, b, channels], weight, None, ALU.mult
+                                )
+                            else:
+                                nc.vector.scalar_tensor_tensor(
+                                    sums[b][:, channels],
+                                    turned[r][:, b, channels],
+                                    weight,
+                                    sums[b][:, channels],
+                                    ALU.mult,
+                                    ALU.add,
+                                )
 
             for b in range(TB):
                 sums_ps = psum_turned.tile([P, P], F32, name="sums_ps", tag="turned")

@@ -26,7 +26,9 @@ TURNED_BANKS = 4
 TURNED_TOGETHER = 2
 AHEAD = 2
 
-VIA_GPSIMD = 3
+VIA_GPSIMD = (1, 4)
+
+VALUES_IN_KEYS_RUN = 2
 
 
 def tile_cantorattention_kernel(tc, x, wq, wkv, bq, bv, offs, out):
@@ -79,19 +81,20 @@ def tile_cantorattention_kernel(tc, x, wq, wkv, bq, bv, offs, out):
                 nc.tensor.matmul(
                     k_ps[:], lhsT=wkv_sb[:, 0:P], rhs=x_sb[:].indirect(piece), start=True, stop=True
                 )
-                slot = "k_sb" if r == R - 1 else f"qk{r}"
+                slot = f"k_sb{VIA_GPSIMD[-1]}" if r == R - 1 else f"qk{r}"
                 qk_r = held.tile([P, S], BF16, name=f"qk{r}", tag=slot)
-                if r == VIA_GPSIMD:
-                    k_sb = held.tile([P, S], F32, name="k_sb")
+                if r in VIA_GPSIMD:
+                    k_sb = held.tile([P, S], F32, name=f"k_sb{r}")
                     nc.scalar.copy(k_sb[:], k_ps[:])
                     nc.gpsimd.tensor_tensor(qk_r[:], k_sb[:], q_sb[:], ALU.mult)
                 else:
                     nc.vector.tensor_tensor(qk_r[:], k_ps[:], q_sb[:], ALU.mult)
                 qk.append(qk_r)
 
-            first_v_ps = psum_keys.tile([P, S], F32, name="first_v_ps", tag="keys")
-            first_values = held.tile([P, S], F32, name="first_values")
-            gather_values(0, first_v_ps, first_values[:])
+            first_values = held.tile([P, VALUES_IN_KEYS_RUN, S], F32, name="first_values")
+            for r in range(VALUES_IN_KEYS_RUN):
+                first_v_ps = psum_keys.tile([P, S], F32, name="first_v_ps", tag="keys")
+                gather_values(r, first_v_ps, first_values[:, r, :])
 
         sc_ps = psum_scores.tile([P, TB, R, H], F32, name="sc_ps")
         for r in range(R):
@@ -126,11 +129,12 @@ def tile_cantorattention_kernel(tc, x, wq, wkv, bq, bv, offs, out):
             tc.psum_pool(name="psum_turned", bufs=TURNED_BANKS) as psum_turned,
         ):
             later_values = held.tile(
-                [P, R - 1, S], F32, name="later_values", tag="shifted_then_values"
+                [P, R - VALUES_IN_KEYS_RUN, S], F32, name="later_values", tag="shifted_then_values"
             )
-            values = [first_values[:]] + [later_values[:, r - 1, :] for r in range(1, R)]
+            values = [first_values[:, r, :] for r in range(VALUES_IN_KEYS_RUN)]
+            values += [later_values[:, r, :] for r in range(R - VALUES_IN_KEYS_RUN)]
             sums = [held.tile([P, P], F32, name=f"sums{b}") for b in range(TB)]
-            gathered = 1
+            gathered = VALUES_IN_KEYS_RUN
             for first in range(0, R, TURNED_TOGETHER):
                 pieces = range(first, first + TURNED_TOGETHER)
                 for r in range(gathered, min(first + TURNED_TOGETHER + AHEAD, R)):

@@ -23,8 +23,9 @@ KEY_BANKS = 7
 VALUE_BANKS = 3
 TURNED_BANKS = 4
 
-TURNED_TOGETHER = 2
-AHEAD = 2
+GATHERED_TOGETHER = 2
+TURNED_TOGETHER = 3
+ROUNDS = 3
 
 VIA_GPSIMD = (1, 4)
 
@@ -133,43 +134,43 @@ def tile_cantorattention_kernel(tc, x, wq, wkv, bq, bv, offs, out):
             )
             values = [first_values[:, r, :] for r in range(VALUES_IN_KEYS_RUN)]
             values += [later_values[:, r, :] for r in range(R - VALUES_IN_KEYS_RUN)]
-            sums = [held.tile([P, P], F32, name=f"sums{b}") for b in range(TB)]
-            gathered = VALUES_IN_KEYS_RUN
-            for first in range(0, R, TURNED_TOGETHER):
-                pieces = range(first, first + TURNED_TOGETHER)
-                for r in range(gathered, min(first + TURNED_TOGETHER + AHEAD, R)):
+            sums = held.tile([P, TB, H, HD], F32, name="sums")
+            for i in range(ROUNDS):
+                first = VALUES_IN_KEYS_RUN + i * GATHERED_TOGETHER
+                for r in range(first, first + GATHERED_TOGETHER):
                     v_ps = psum_values.tile([P, S], F32, name="v_ps")
                     gather_values(r, v_ps, values[r])
-                    gathered = r + 1
-                turned = {}
-                for r in pieces:
-                    turned[r] = psum_turned.tile([P, TB, P], F32, name="turned", tag="turned")
+                stop = R - (ROUNDS - 1 - i) * TURNED_TOGETHER
+                for r in range(max(stop - TURNED_TOGETHER, 0), stop):
+                    turned = psum_turned.tile([P, TB, P], F32, name="turned", tag="turned")
                     for b in range(TB):
                         nc.tensor.transpose(
-                            turned[r][:, b, :], values[r][:, b * P : (b + 1) * P], identity[:]
+                            turned[:, b, :], values[r][:, b * P : (b + 1) * P], identity[:]
                         )
-                for r in pieces:
+                    if r == 0:
+                        nc.vector.tensor_tensor(
+                            sums[:],
+                            turned[:].rearrange("t b (h c) -> t b h c", h=H),
+                            p[:, :, r, :].unsqueeze(3).to_broadcast([P, TB, H, HD]),
+                            ALU.mult,
+                        )
+                        continue
                     for b in range(TB):
                         for h in range(H):
-                            channels = slice(h * HD, (h + 1) * HD)
-                            weight = p[:, b, r, h : h + 1]
-                            if r == 0:
-                                nc.vector.tensor_scalar(
-                                    sums[b][:, channels], turned[r][:, b, channels], weight, None, ALU.mult
-                                )
-                            else:
-                                nc.vector.scalar_tensor_tensor(
-                                    sums[b][:, channels],
-                                    turned[r][:, b, channels],
-                                    weight,
-                                    sums[b][:, channels],
-                                    ALU.mult,
-                                    ALU.add,
-                                )
+                            nc.vector.scalar_tensor_tensor(
+                                sums[:, b, h, :],
+                                turned[:, b, h * HD : (h + 1) * HD],
+                                p[:, b, r, h : h + 1],
+                                sums[:, b, h, :],
+                                ALU.mult,
+                                ALU.add,
+                            )
 
             for b in range(TB):
                 sums_ps = psum_turned.tile([P, P], F32, name="sums_ps", tag="turned")
-                nc.tensor.transpose(sums_ps[:], sums[b][:], identity[:])
+                nc.tensor.transpose(
+                    sums_ps[:], sums[:, b, :, :].rearrange("t h c -> t (h c)"), identity[:]
+                )
                 out_sb = held.tile([P, P], F32, name=f"out_sb{b}")
                 if b % 2 == 0:
                     nc.scalar.activation(out_sb[:], sums_ps[:], ACT.Identity, bias=bv_sb[:])

@@ -134,7 +134,7 @@ def tile_cantorattention_kernel(tc, x, wq, wkv, bq, bv, offs, out):
             )
             values = [first_values[:, r, :] for r in range(VALUES_IN_KEYS_RUN)]
             values += [later_values[:, r, :] for r in range(R - VALUES_IN_KEYS_RUN)]
-            sums = held.tile([P, TB, H, HD], F32, name="sums")
+            sums = [held.tile([P, P], F32, name=f"sums{b}") for b in range(TB)]
             for i in range(ROUNDS):
                 first = VALUES_IN_KEYS_RUN + i * GATHERED_TOGETHER
                 for r in range(first, first + GATHERED_TOGETHER):
@@ -147,30 +147,27 @@ def tile_cantorattention_kernel(tc, x, wq, wkv, bq, bv, offs, out):
                         nc.tensor.transpose(
                             turned[:, b, :], values[r][:, b * P : (b + 1) * P], identity[:]
                         )
-                    if r == 0:
-                        nc.vector.tensor_tensor(
-                            sums[:],
-                            turned[:].rearrange("t b (h c) -> t b h c", h=H),
-                            p[:, :, r, :].unsqueeze(3).to_broadcast([P, TB, H, HD]),
-                            ALU.mult,
-                        )
-                        continue
                     for b in range(TB):
                         for h in range(H):
-                            nc.vector.scalar_tensor_tensor(
-                                sums[:, b, h, :],
-                                turned[:, b, h * HD : (h + 1) * HD],
-                                p[:, b, r, h : h + 1],
-                                sums[:, b, h, :],
-                                ALU.mult,
-                                ALU.add,
-                            )
+                            channels = slice(h * HD, (h + 1) * HD)
+                            weight = p[:, b, r, h : h + 1]
+                            if r == 0:
+                                nc.vector.tensor_scalar(
+                                    sums[b][:, channels], turned[:, b, channels], weight, None, ALU.mult
+                                )
+                            else:
+                                nc.vector.scalar_tensor_tensor(
+                                    sums[b][:, channels],
+                                    turned[:, b, channels],
+                                    weight,
+                                    sums[b][:, channels],
+                                    ALU.mult,
+                                    ALU.add,
+                                )
 
             for b in range(TB):
                 sums_ps = psum_turned.tile([P, P], F32, name="sums_ps", tag="turned")
-                nc.tensor.transpose(
-                    sums_ps[:], sums[:, b, :, :].rearrange("t h c -> t (h c)"), identity[:]
-                )
+                nc.tensor.transpose(sums_ps[:], sums[b][:], identity[:])
                 out_sb = held.tile([P, P], F32, name=f"out_sb{b}")
                 if b % 2 == 0:
                     nc.scalar.activation(out_sb[:], sums_ps[:], ACT.Identity, bias=bv_sb[:])

import concourse.mybir as mybir
from concourse.masks import make_identity

F32 = mybir.dt.float32
BF16 = mybir.dt.bfloat16
U16 = mybir.dt.uint16
ALU = mybir.AluOpType
ACT = mybir.ActivationFunctionType
AX = mybir.AxisListType

P = 128
S = 512
R = 8
H = 2
HD = P // H
TB = S // P
PIECE_COLS = S // 16
SCALE = 0.125

FLOPS = 2 * P * (2 * P) * (R * S) + 2 * P * P * S + 4 * P * R * S

KEY_BANKS = 7
VALUE_BANKS = 3
TURNED_BANKS = 4

GATHERED_TOGETHER = 2
TURNED_TOGETHER = 3
ROUNDS = 3

VIA_GPSIMD = (1, 4)

VALUES_IN_KEYS_RUN = 2


def tile_cantorattention_kernel(tc, x, wq, wkv, bq, bv, offs, out):
    nc = tc.nc
    with (
        tc.tile_pool(name="held", bufs=1) as held,
        tc.psum_pool(name="psum_scores", bufs=1) as psum_scores,
    ):
        wq_sb = held.tile([P, P], BF16, name="wq_sb")
        nc.sync.dma_start(wq_sb[:], wq)
        x_sb = held.tile([P, S], BF16, name="x_sb")
        nc.scalar.dma_start(x_sb[:], x)
        offsets = held.tile([P, R * PIECE_COLS], U16, name="offsets")
        nc.sync.dma_start(offsets[:], offs)
        wkv_sb = held.tile([P, 2 * P], BF16, name="wkv_sb")
        nc.scalar.dma_start(wkv_sb[:], wkv)
        bq_sb = held.tile([P, 1], F32, name="bq_sb")
        nc.sync.dma_start(bq_sb[:], bq)
        bv_sb = held.tile([P, 1], F32, name="bv_sb")
        nc.scalar.dma_start(bv_sb[:], bv)

        warm = held.tile([P, 1], F32, name="warm")
        nc.vector.memset(warm[:], 0.0)
        nc.scalar.activation(warm[:], warm[:], ACT.Exp)

        head_of = held.tile([P, H], BF16, name="head_of")
        nc.vector.memset(head_of[:], 0.0)
        for h in range(H):
            nc.vector.memset(head_of[h * HD : (h + 1) * HD, h : h + 1], 1.0)

        identity = held.tile([P, P], F32, name="identity")
        make_identity(nc, identity[:])

        def gather_values(r, v_ps, v_sb):
            piece = offsets[:, r * PIECE_COLS : (r + 1) * PIECE_COLS]
            nc.tensor.matmul(
                v_ps[:], lhsT=wkv_sb[:, P : 2 * P], rhs=x_sb[:].indirect(piece), start=True, stop=True
            )
            nc.scalar.copy(v_sb, v_ps[:])

        qk = []
        with tc.psum_pool(name="psum_keys", bufs=KEY_BANKS) as psum_keys:
            q_ps = psum_keys.tile([P, S], F32, name="q_ps", tag="keys")
            nc.tensor.matmul(q_ps[:], lhsT=wq_sb[:], rhs=x_sb[:], start=True, stop=True)
            q_sb = held.tile([P, S], F32, name="q_sb")
            nc.scalar.activation(q_sb[:], q_ps[:], ACT.Identity, bias=bq_sb[:])
            for r in range(R):
                piece = offsets[:, r * PIECE_COLS : (r + 1) * PIECE_COLS]
                k_ps = psum_keys.tile([P, S], F32, name="k_ps", tag="keys")
                nc.tensor.matmul(
                    k_ps[:], lhsT=wkv_sb[:, 0:P], rhs=x_sb[:].indirect(piece), start=True, stop=True
                )
                slot = f"k_sb{VIA_GPSIMD[-1]}" if r == R - 1 else f"qk{r}"
                qk_r = held.tile([P, S], BF16, name=f"qk{r}", tag=slot)
                if r in VIA_GPSIMD:
                    k_sb = held.tile([P, S], F32, name=f"k_sb{r}")
                    nc.scalar.copy(k_sb[:], k_ps[:])
                    nc.gpsimd.tensor_tensor(qk_r[:], k_sb[:], q_sb[:], ALU.mult)
                else:
                    nc.vector.tensor_tensor(qk_r[:], k_ps[:], q_sb[:], ALU.mult)
                qk.append(qk_r)

            first_values = held.tile([P, VALUES_IN_KEYS_RUN, S], F32, name="first_values")
            for r in range(VALUES_IN_KEYS_RUN):
                first_v_ps = psum_keys.tile([P, S], F32, name="first_v_ps", tag="keys")
                gather_values(r, first_v_ps, first_values[:, r, :])

        sc_ps = psum_scores.tile([P, TB, R, H], F32, name="sc_ps")
        for r in range(R):
            for b in range(TB):
                nc.tensor.matmul(
                    sc_ps[:, b, r, :],
                    lhsT=qk[r][:, b * P : (b + 1) * P],
                    rhs=head_of[:],
                    start=True,
                    stop=True,
                )

        top = held.tile([P, TB, H], F32, name="top")
        nc.vector.reduce_max(top[:], sc_ps[:].rearrange("t b r h -> t b h r"), axis=AX.X)
        shifted = held.tile([P, TB, R, H], F32, name="shifted", tag="shifted_then_values")
        nc.vector.tensor_tensor(
            shifted[:], sc_ps[:], top[:].unsqueeze(2).to_broadcast([P, TB, R, H]), ALU.subtract
        )
        e = held.tile([P, TB, R, H], F32, name="e")
        nc.scalar.activation(e[:], shifted[:], ACT.Exp, scale=SCALE)
        den = held.tile([P, TB, H], F32, name="den")
        nc.vector.reduce_sum(den[:], e[:].rearrange("t b r h -> t b h r"), axis=AX.X)
        rden = held.tile([P, TB, H], F32, name="rden")
        nc.vector.reciprocal(rden[:], den[:])
        p = held.tile([P, TB, R, H], F32, name="p")
        nc.vector.tensor_tensor(
            p[:], e[:], rden[:].unsqueeze(2).to_broadcast([P, TB, R, H]), ALU.mult
        )

        with (
            tc.psum_pool(name="psum_values", bufs=VALUE_BANKS) as psum_values,
            tc.psum_pool(name="psum_turned", bufs=TURNED_BANKS) as psum_turned,
        ):
            later_values = held.tile(
                [P, R - VALUES_IN_KEYS_RUN, S], F32, name="later_values", tag="shifted_then_values"
            )
            values = [first_values[:, r, :] for r in range(VALUES_IN_KEYS_RUN)]
            values += [later_values[:, r, :] for r in range(R - VALUES_IN_KEYS_RUN)]
            sums = [held.tile([P, P], F32, name=f"sums{b}") for b in range(TB)]
            for i in range(ROUNDS):
                first = VALUES_IN_KEYS_RUN + i * GATHERED_TOGETHER
                for r in range(first, first + GATHERED_TOGETHER):
                    v_ps = psum_values.tile([P, S], F32, name="v_ps")
                    gather_values(r, v_ps, values[r])
                stop = R - (ROUNDS - 1 - i) * TURNED_TOGETHER
                for r in range(max(stop - TURNED_TOGETHER, 0), stop):
                    turned = psum_turned.tile([P, TB, P], F32, name="turned", tag="turned")
                    for b in range(TB):
                        nc.tensor.transpose(
                            turned[:, b, :], values[r][:, b * P : (b + 1) * P], identity[:]
                        )
                    for b in range(TB):
                        for h in range(H):
                            channels = slice(h * HD, (h + 1) * HD)
                            weight = p[:, b, r, h : h + 1]
                            if r == 0:
                                nc.vector.tensor_scalar(
                                    sums[b][:, channels], turned[:, b, channels], weight, None, ALU.mult
                                )
                            else:
                                nc.vector.scalar_tensor_tensor(
                                    sums[b][:, channels],
                                    turned[:, b, channels],
                                    weight,
                                    sums[b][:, channels],
                                    ALU.mult,
                                    ALU.add,
                                )

            for b in range(TB):
                sums_ps = psum_turned.tile([P, P], F32, name="sums_ps", tag="turned")
                nc.tensor.transpose(sums_ps[:], sums[b][:], identity[:])
                out_sb = held.tile([P, P], F32, name=f"out_sb{b}")
                if b % 2 == 0:
                    nc.scalar.activation(out_sb[:], sums_ps[:], ACT.Identity, bias=bv_sb[:])
                else:
                    nc.vector.tensor_scalar(out_sb[:], sums_ps[:], bv_sb[:], None, ALU.add)
                nc.sync.dma_start(out[:, b * P : (b + 1) * P], out_sb[:])
